import numpy as np
import ml_dtypes


def mxq(x, axis, fmt="e4m3"):
    dtype, down = {"e4m3": (ml_dtypes.float8_e4m3fn, 7), "e5m2": (ml_dtypes.float8_e5m2, 14)}[fmt]
    v = np.moveaxis(np.asarray(x, np.float32).astype(ml_dtypes.bfloat16).astype(np.float64), axis, -1)
    blocks = v.reshape(v.shape[:-1] + (-1, 32))
    amax = np.abs(blocks).max(-1, keepdims=True)
    byte = np.maximum(np.where(amax > 0, np.frexp(amax)[1] - 1 + 127, 0) - down, 1)
    scale = np.exp2(byte - 127.0)
    codes = (blocks / scale).astype(np.float32).astype(dtype).astype(np.float64)
    return np.moveaxis((codes * scale).reshape(v.shape), -1, axis)


WIDE = False


def mx_kscale(k):
    if not WIDE:
        return np.ones(k)
    levels = np.array([10, -10, 5, -5, 0])
    a = np.random.permutation(np.resize(levels, k // 512 * 4)).reshape(k // 512, 4)
    idx = np.arange(k)
    return np.exp2(a[idx // 512, idx % 128 // 32])


BF16 = ml_dtypes.bfloat16


def bf(x):
    return np.asarray(x, np.float32).astype(BF16)


def f64(x):
    return np.asarray(x).astype(np.float64)


B, HW, C, HID, WS, SS, HEADS = 4, 32, 512, 2048, 8, 4, 8
L = HW * HW
NH = HW // WS
HD = C // HEADS
EPS = 1e-5


def ln(x, w, b):
    m = x.mean(-1, keepdims=True)
    xm = x - m
    v = np.mean(xm * xm, axis=-1, keepdims=True)
    return xm * (1.0 / np.sqrt(v + EPS)) * w + b


def setup_inputs():
    s = mx_kscale(C)
    return {"x": bf(np.random.standard_normal((B, L, C))),
            "ln1_w": bf((1.0 + 0.1 * np.random.standard_normal(C)) * s),
            "ln1_b": bf(0.1 * np.random.standard_normal(C) * s),
            "in_proj_w": bf(np.random.standard_normal((3 * C, C)) / np.sqrt(C) / s[None, :]),
            "in_proj_b": bf(0.1 * np.random.standard_normal(3 * C))}


def reference(x, ln1_w, ln1_b, in_proj_w, in_proj_b):
    h = ln(f64(x), f64(ln1_w), f64(ln1_b)).reshape(B, HW, HW, C)
    h = np.roll(h, (-SS, -SS), axis=(1, 2))
    win = np.swapaxes(h.reshape(B, NH, WS, NH, WS, C), 2, 3).reshape(-1, WS * WS, C)
    win = win
    qkv = (mxq(win, 2, "e4m3") @ mxq(f64(in_proj_w), 1, "e4m3").T) + f64(in_proj_b)
    q, k, v = np.split(qkv, 3, axis=-1)
    S, N = win.shape[0], win.shape[1]
    q = q.reshape(S, N, HEADS, HD) * (HD ** -0.5)
    k = k.reshape(S, N, HEADS, HD)
    v = v.reshape(S, N, HEADS, HD)
    return q, k, v

@@ -1,0 +1,246 @@
+import concourse.mybir as mybir
+from concourse.masks import make_identity
+
+F32 = mybir.dt.float32
+BF16 = mybir.dt.bfloat16
+U32 = mybir.dt.uint32
+U8 = mybir.dt.uint8
+FP8X4 = mybir.dt.float8_e4m3fn_x4
+ACT = mybir.ActivationFunctionType
+ALU = mybir.AluOpType
+
+P = 128
+PACK = 4
+C = P * PACK
+BATCHES = 4
+SLOTS = 8
+GROUP = 4
+HALVES = SLOTS // GROUP
+GROUPS = BATCHES * HALVES
+GRID = 32
+WINDOW = 8
+SHIFT = 4
+WINDOWS = GRID // WINDOW
+N_OUT = 3
+ROW_TILES = C // P
+EPS = 1e-5
+OUT_SCALE = (64.0**-0.5, 1.0, 1.0)
+
+FLOPS = 2 * BATCHES * GRID * GRID * C * N_OUT * C
+
+
+def tile_swintransformerblock_pa_t_kernel(
+    tc, x, ln1_w, ln1_b, in_proj_w, in_proj_b, out_0, out_1, out_2
+):
+    nc = tc.nc
+
+    x_view = x.rearrange("b (p e) c -> b p e c", e=SLOTS)
+    w_view = in_proj_w.rearrange("(a p) k -> p a k", p=P)
+    out_views = [
+        o.rearrange("w n h d -> (w n) (h d)").rearrange("(b p e) k -> b p e k", b=BATCHES, e=SLOTS)
+        for o in (out_0, out_1, out_2)
+    ]
+
+    with (
+        tc.tile_pool(name="const", bufs=1) as const,
+        tc.tile_pool(name="small", bufs=3) as small,
+        tc.tile_pool(name="work", bufs=2) as work,
+        tc.tile_pool(name="stage", bufs=2) as stage,
+        tc.psum_pool(name="psum_t", bufs=4) as psum_t,
+        tc.psum_pool(name="psum_acc", bufs=4) as psum_acc,
+    ):
+        def first_slot(half):
+            return (SHIFT + GROUP * half) % SLOTS
+
+        x_tiles = []
+        w_raw = []
+        for g in range(GROUPS):
+            x_tiles.append(const.tile([P, GROUP, C], BF16, name="x_%d" % g))
+        for n in range(N_OUT):
+            w_raw.append(const.tile([P, ROW_TILES, C], BF16, name="w_raw_%d" % n))
+
+        def load_x(g):
+            batch, half = divmod(g, HALVES)
+            e0 = first_slot(half)
+            nc.sync.dma_start(out=x_tiles[g][:], in_=x_view[batch][:, e0 : e0 + GROUP, :])
+
+        load_x(0)
+        for n in range(N_OUT):
+            nc.sync.dma_start(out=w_raw[n][:], in_=w_view[:, n * ROW_TILES : (n + 1) * ROW_TILES, :])
+        for g in range(1, GROUPS):
+            load_x(g)
+
+        norm_rows = const.tile([P, P], BF16)
+        nc.vector.memset(norm_rows[:], 0.0)
+        nc.scalar.dma_start(out=norm_rows[0:PACK, :], in_=ln1_w.rearrange("(t p) -> t p", p=P))
+        nc.scalar.dma_start(out=norm_rows[PACK : 2 * PACK, :], in_=ln1_b.rearrange("(t p) -> t p", p=P))
+        bias_row = const.tile([P, N_OUT * C], BF16)
+        nc.vector.memset(bias_row[:], 0.0)
+        nc.scalar.dma_start(out=bias_row[0:1, :], in_=in_proj_b.rearrange("(o n) -> o n", o=1))
+
+        ident_f32 = const.tile([P, P], F32)
+        make_identity(nc, ident_f32[:])
+        ident_bf16 = const.tile([P, P], BF16)
+        nc.vector.tensor_copy(out=ident_bf16[:], in_=ident_f32[:])
+        ones = const.tile([P, P], BF16)
+        nc.vector.memset(ones[:], 1.0)
+        eps = const.tile([P, 1], F32)
+        nc.vector.memset(eps[:], EPS)
+
+        rolled = const.tile([P, P], F32)
+        turn = SHIFT * WINDOWS
+        nc.vector.tensor_copy(out=rolled[:, 0 : P - turn], in_=ident_f32[:, turn:P])
+        nc.vector.tensor_copy(out=rolled[:, P - turn : P], in_=ident_f32[:, 0:turn])
+        perm = const.tile([P, HALVES, P], F32)
+        rolled_v = rolled[:].rearrange("p (wi r jq) -> p wi jq r", wi=WINDOWS, r=WINDOW)
+        perm_0 = perm[:, 0, :].rearrange("p (wi wj r) -> p wi wj r", wi=WINDOWS, r=WINDOW)
+        perm_1 = perm[:, 1, :].rearrange("p (wi wj r) -> p wi wj r", wi=WINDOWS, r=WINDOW)
+        nc.vector.tensor_copy(out=perm_0, in_=rolled_v)
+        nc.vector.tensor_copy(out=perm_1[:, :, 0 : WINDOWS - 1, :], in_=rolled_v[:, :, 1:WINDOWS, :])
+        nc.vector.tensor_copy(out=perm_1[:, :, WINDOWS - 1 : WINDOWS, :], in_=rolled_v[:, :, 0:1, :])
+
+        norm_cols_ps = psum_t.tile([P, P], BF16, tag="xt")
+        nc.tensor.transpose(norm_cols_ps[:], norm_rows[:], ident_bf16[:])
+        norm_cols = const.tile([P, 2 * PACK], F32)
+        nc.vector.tensor_copy(out=norm_cols[:], in_=norm_cols_ps[:, 0 : 2 * PACK])
+
+        bias_all = const.tile([P, N_OUT, C], F32)
+        for n in range(N_OUT):
+            bias_ps = psum_acc.tile([P, C], F32, tag="acc")
+            nc.tensor.matmul(bias_ps[:], lhsT=ones[:], rhs=bias_row[:, n * C : (n + 1) * C], start=True, stop=True)
+            nc.scalar.activation(out=bias_all[:, n, :], in_=bias_ps[:], func=ACT.Copy, scale=OUT_SCALE[n])
+
+        w_codes = const.tile([P, N_OUT * C], U32, align_bytes=64)
+        w_scales = const.tile([P, N_OUT * C], U8, align_bytes=64)
+
+        def quantise_weights(n):
+            w_grouped = work.tile([P, C, PACK], BF16, align_bytes=64)
+            for pair in range(ROW_TILES // 2):
+                wt = psum_t.tile([P, 2, PACK, P], BF16, tag="xt")
+                for a in range(2):
+                    for t in range(PACK):
+                        nc.tensor.transpose(
+                            wt[:, a, t, :], w_raw[n][:, 2 * pair + a, t * P : (t + 1) * P], ident_bf16[:]
+                        )
+                dst = w_grouped[:, 2 * pair * P : 2 * (pair + 1) * P, :].rearrange("p (a o) t -> p a o t", a=2)
+                src = wt[:].rearrange("p a t o -> p a o t")
+                if pair % 2 == 0:
+                    nc.vector.tensor_copy(out=dst, in_=src)
+                else:
+                    nc.scalar.copy(out=dst, in_=src)
+            nc.vector.quantize_mx(
+                out=w_codes[:, n * C : (n + 1) * C].bitcast(FP8X4),
+                scales=w_scales[:, n * C : (n + 1) * C],
+                in_=w_grouped[:].rearrange("p o t -> p (o t)"),
+            )
+
+        moments = {}
+        normed = {}
+        chunks = {}
+        quantised = {}
+
+        def statistics(g):
+            stats = small.tile([P, GROUP, 6], F32)
+            for j in range(GROUP):
+                nc.vector.bn_stats(out=stats[:, j, :], in_=x_tiles[g][:, j, :])
+            mean_var = small.tile([P, GROUP, 2], F32)
+            for j in range(GROUP):
+                nc.vector.bn_aggr(out=mean_var[:, j, :], in_=stats[:, j, :])
+            std = small.tile([P, GROUP], F32)
+            nc.scalar.activation(out=std[:], in_=mean_var[:, :, 1], func=ACT.Sqrt, bias=eps[:, 0:1], scale=1.0)
+            rstd = small.tile([P, GROUP], F32)
+            nc.vector.reciprocal(out=rstd[:], in_=std[:])
+            shift = small.tile([P, GROUP], F32)
+            nc.vector.scalar_tensor_tensor(
+                out=shift[:], in0=mean_var[:, :, 0], scalar=-1.0, in1=rstd[:], op0=ALU.mult, op1=ALU.mult
+            )
+            moments[g] = (rstd, shift)
+
+        def normalise(g):
+            rstd, shift = moments[g]
+            xn = work.tile([P, GROUP, C], F32)
+            for j in range(GROUP):
+                nc.scalar.activation(
+                    out=xn[:, j, :],
+                    in_=x_tiles[g][:, j, :],
+                    func=ACT.Identity,
+                    scale=rstd[:, j : j + 1],
+                    bias=shift[:, j : j + 1],
+                )
+            normed[g] = xn
+
+        def transpose_and_scale(g):
+            half = g % HALVES
+            h_chunks = work.tile([P, PACK, GROUP * P], BF16)
+            for t in range(PACK):
+                xt = psum_t.tile([P, GROUP, P], F32, tag="xt")
+                for j in range(GROUP):
+                    nc.tensor.transpose(xt[:, j, :], normed[g][:, j, t * P : (t + 1) * P], perm[:, half, :])
+                nc.scalar.activation(
+                    out=h_chunks[:, t, :],
+                    in_=xt[:].rearrange("p j m -> p (j m)"),
+                    func=ACT.Identity,
+                    scale=norm_cols[:, t : t + 1],
+                    bias=norm_cols[:, PACK + t : PACK + t + 1],
+                )
+            chunks[g] = h_chunks
+
+        def group_and_quantise(g):
+            h_grouped = work.tile([P, GROUP * P, PACK], BF16, align_bytes=64)
+            nc.vector.tensor_copy(
+                out=h_grouped[:].rearrange("p (m i) t -> p m t i", i=4),
+                in_=chunks[g][:].rearrange("p t (m i) -> p m t i", i=4),
+            )
+            codes = work.tile([P, GROUP * P], U32, align_bytes=64)
+            scales = work.tile([P, GROUP * P], U8, align_bytes=64)
+            nc.vector.quantize_mx(
+                out=codes[:].bitcast(FP8X4), scales=scales[:], in_=h_grouped[:].rearrange("p m t -> p (m t)")
+            )
+            quantised[g] = (codes, scales)
+
+        def project(g):
+            batch, half = divmod(g, HALVES)
+            codes, scales = quantised[g]
+            results = [stage.tile([P, GROUP, C], F32, name="result_%d" % n) for n in range(N_OUT)]
+            for j in range(GROUP):
+                for n in range(N_OUT):
+                    acc = psum_acc.tile([P, C], F32, tag="acc")
+                    nc.tensor.matmul_mx(
+                        out=acc[:],
+                        lhsT=codes[:, j * P : (j + 1) * P].bitcast(FP8X4),
+                        lhsT_scale=scales[:, j * P : (j + 1) * P],
+                        rhs=w_codes[:, n * C : (n + 1) * C].bitcast(FP8X4),
+                        rhs_scale=w_scales[:, n * C : (n + 1) * C],
+                        start=True,
+                        stop=True,
+                    )
+                    piece = results[n][:, j, :]
+                    if (j * N_OUT + n) % 2 == 0:
+                        nc.vector.scalar_tensor_tensor(
+                            out=piece, in0=acc[:], scalar=OUT_SCALE[n], in1=bias_all[:, n, :], op0=ALU.mult, op1=ALU.add
+                        )
+                    else:
+                        nc.scalar.activation(out=piece, in_=acc[:], func=ACT.Copy, scale=OUT_SCALE[n])
+                        nc.gpsimd.tensor_tensor(out=piece, in0=piece, in1=bias_all[:, n, :], op=ALU.add)
+            place0 = GROUP * half
+            for n in range(N_OUT):
+                nc.sync.dma_start(out=out_views[n][batch][:, place0 : place0 + GROUP, :], in_=results[n][:])
+
+        statistics(0)
+        normalise(0)
+        for n in range(N_OUT):
+            quantise_weights(n)
+        transpose_and_scale(0)
+        statistics(1)
+        group_and_quantise(0)
+        normalise(1)
+        for g in range(GROUPS):
+            project(g)
+            if g + 1 < GROUPS:
+                transpose_and_scale(g + 1)
+            if g + 2 < GROUPS:
+                statistics(g + 2)
+            if g + 1 < GROUPS:
+                group_and_quantise(g + 1)
+            if g + 2 < GROUPS:
+                normalise(g + 2)

@@ -16,6 +16,7 @@ BATCHES = 4
 SLOTS = 8
 GROUP = 4
 HALVES = SLOTS // GROUP
+STORE_TILES = 2
 GROUPS = BATCHES * HALVES
 GRID = 32
 WINDOW = 8
@@ -43,9 +44,9 @@ def tile_swintransformerblock_pa_t_kernel(
 
     with (
         tc.tile_pool(name="const", bufs=1) as const,
-        tc.tile_pool(name="small", bufs=3) as small,
+        tc.tile_pool(name="small", bufs=4) as small,
         tc.tile_pool(name="work", bufs=2) as work,
-        tc.tile_pool(name="stage", bufs=2) as stage,
+        tc.tile_pool(name="stage", bufs=4) as stage,
         tc.psum_pool(name="psum_t", bufs=4) as psum_t,
         tc.psum_pool(name="psum_acc", bufs=4) as psum_acc,
     ):
@@ -187,7 +188,7 @@ def tile_swintransformerblock_pa_t_kernel(
 
         def group_and_quantise(g):
             h_grouped = work.tile([P, GROUP * P, PACK], BF16, align_bytes=64)
-            nc.vector.tensor_copy(
+            nc.scalar.copy(
                 out=h_grouped[:].rearrange("p (m i) t -> p m t i", i=4),
                 in_=chunks[g][:].rearrange("p t (m i) -> p m t i", i=4),
             )
@@ -201,30 +202,34 @@ def tile_swintransformerblock_pa_t_kernel(
         def project(g):
             batch, half = divmod(g, HALVES)
             codes, scales = quantised[g]
-            results = [stage.tile([P, GROUP, C], F32, name="result_%d" % n) for n in range(N_OUT)]
-            for j in range(GROUP):
-                for n in range(N_OUT):
-                    acc = psum_acc.tile([P, C], F32, tag="acc")
-                    nc.tensor.matmul_mx(
-                        out=acc[:],
-                        lhsT=codes[:, j * P : (j + 1) * P].bitcast(FP8X4),
-                        lhsT_scale=scales[:, j * P : (j + 1) * P],
-                        rhs=w_codes[:, n * C : (n + 1) * C].bitcast(FP8X4),
-                        rhs_scale=w_scales[:, n * C : (n + 1) * C],
-                        start=True,
-                        stop=True,
-                    )
-                    piece = results[n][:, j, :]
-                    if (j * N_OUT + n) % 2 == 0:
-                        nc.vector.scalar_tensor_tensor(
-                            out=piece, in0=acc[:], scalar=OUT_SCALE[n], in1=bias_all[:, n, :], op0=ALU.mult, op1=ALU.add
+            for first in range(0, GROUP, STORE_TILES):
+                results = [stage.tile([P, STORE_TILES, C], F32, name="result_%d" % n) for n in range(N_OUT)]
+                for i in range(STORE_TILES):
+                    j = first + i
+                    for n in range(N_OUT):
+                        acc = psum_acc.tile([P, C], F32, tag="acc")
+                        nc.tensor.matmul_mx(
+                            out=acc[:],
+                            lhsT=codes[:, j * P : (j + 1) * P].bitcast(FP8X4),
+                            lhsT_scale=scales[:, j * P : (j + 1) * P],
+                            rhs=w_codes[:, n * C : (n + 1) * C].bitcast(FP8X4),
+                            rhs_scale=w_scales[:, n * C : (n + 1) * C],
+                            start=True,
+                            stop=True,
                         )
-                    else:
-                        nc.scalar.activation(out=piece, in_=acc[:], func=ACT.Copy, scale=OUT_SCALE[n])
-                        nc.gpsimd.tensor_tensor(out=piece, in0=piece, in1=bias_all[:, n, :], op=ALU.add)
-            place0 = GROUP * half
-            for n in range(N_OUT):
-                nc.sync.dma_start(out=out_views[n][batch][:, place0 : place0 + GROUP, :], in_=results[n][:])
+                        nc.vector.scalar_tensor_tensor(
+                            out=results[n][:, i, :],
+                            in0=acc[:],
+                            scalar=OUT_SCALE[n],
+                            in1=bias_all[:, n, :],
+                            op0=ALU.mult,
+                            op1=ALU.add,
+                        )
+                place0 = GROUP * half + first
+                for n in range(N_OUT):
+                    nc.sync.dma_start(
+                        out=out_views[n][batch][:, place0 : place0 + STORE_TILES, :], in_=results[n][:]
+                    )
 
         statistics(0)
         normalise(0)

@@ -16,8 +16,8 @@ BATCHES = 4
 SLOTS = 8
 GROUP = 4
 HALVES = SLOTS // GROUP
-STORE_TILES = 2
 GROUPS = BATCHES * HALVES
+STORE_TILES = 2
 GRID = 32
 WINDOW = 8
 SHIFT = 4
@@ -26,6 +26,7 @@ N_OUT = 3
 ROW_TILES = C // P
 EPS = 1e-5
 OUT_SCALE = (64.0**-0.5, 1.0, 1.0)
+AHEAD = 4
 
 FLOPS = 2 * BATCHES * GRID * GRID * C * N_OUT * C
 
@@ -44,31 +45,30 @@ def tile_swintransformerblock_pa_t_kernel(
 
     with (
         tc.tile_pool(name="const", bufs=1) as const,
-        tc.tile_pool(name="small", bufs=4) as small,
+        tc.tile_pool(name="small", bufs=AHEAD) as small,
         tc.tile_pool(name="work", bufs=2) as work,
         tc.tile_pool(name="stage", bufs=4) as stage,
         tc.psum_pool(name="psum_t", bufs=4) as psum_t,
         tc.psum_pool(name="psum_acc", bufs=4) as psum_acc,
+        tc.manual_schedule(),
     ):
-        def first_slot(half):
-            return (SHIFT + GROUP * half) % SLOTS
-
-        x_tiles = []
-        w_raw = []
-        for g in range(GROUPS):
-            x_tiles.append(const.tile([P, GROUP, C], BF16, name="x_%d" % g))
-        for n in range(N_OUT):
-            w_raw.append(const.tile([P, ROW_TILES, C], BF16, name="w_raw_%d" % n))
+        x_tiles = [const.tile([P, GROUP, C], BF16, name="x_%d" % g) for g in range(GROUPS)]
+        w_raw = [const.tile([P, ROW_TILES, C], BF16, name="w_raw_%d" % n) for n in range(N_OUT)]
 
         def load_x(g):
             batch, half = divmod(g, HALVES)
-            e0 = first_slot(half)
-            nc.sync.dma_start(out=x_tiles[g][:], in_=x_view[batch][:, e0 : e0 + GROUP, :])
+            slot0 = (SHIFT + GROUP * half) % SLOTS
+            nc.sync.dma_start(out=x_tiles[g][:], in_=x_view[batch][:, slot0 : slot0 + GROUP, :])
+
+        def load_w(n):
+            nc.sync.dma_start(out=w_raw[n][:], in_=w_view[:, n * ROW_TILES : (n + 1) * ROW_TILES, :])
 
         load_x(0)
-        for n in range(N_OUT):
-            nc.sync.dma_start(out=w_raw[n][:], in_=w_view[:, n * ROW_TILES : (n + 1) * ROW_TILES, :])
-        for g in range(1, GROUPS):
+        load_w(0)
+        load_x(1)
+        load_w(1)
+        load_w(2)
+        for g in range(2, GROUPS):
             load_x(g)
 
         norm_rows = const.tile([P, P], BF16)
@@ -113,90 +113,129 @@ def tile_swintransformerblock_pa_t_kernel(
 
         w_codes = const.tile([P, N_OUT * C], U32, align_bytes=64)
         w_scales = const.tile([P, N_OUT * C], U8, align_bytes=64)
+        w_grouped = {}
 
-        def quantise_weights(n):
-            w_grouped = work.tile([P, C, PACK], BF16, align_bytes=64)
+        def transpose_weights(n):
+            w_grouped[n] = work.tile([P, C, PACK], BF16, align_bytes=64, name="w_grouped")
             for pair in range(ROW_TILES // 2):
-                wt = psum_t.tile([P, 2, PACK, P], BF16, tag="xt")
+                wt = psum_acc.tile([P, 2, PACK, P], BF16, tag="acc")
                 for a in range(2):
                     for t in range(PACK):
                         nc.tensor.transpose(
                             wt[:, a, t, :], w_raw[n][:, 2 * pair + a, t * P : (t + 1) * P], ident_bf16[:]
                         )
-                dst = w_grouped[:, 2 * pair * P : 2 * (pair + 1) * P, :].rearrange("p (a o) t -> p a o t", a=2)
-                src = wt[:].rearrange("p a t o -> p a o t")
-                if pair % 2 == 0:
-                    nc.vector.tensor_copy(out=dst, in_=src)
-                else:
-                    nc.scalar.copy(out=dst, in_=src)
+                nc.scalar.copy(
+                    out=w_grouped[n][:, 2 * pair * P : 2 * (pair + 1) * P, :].rearrange("p (a o) t -> p a o t", a=2),
+                    in_=wt[:].rearrange("p a t o -> p a o t"),
+                )
+
+        def quantise_weights(n):
             nc.vector.quantize_mx(
                 out=w_codes[:, n * C : (n + 1) * C].bitcast(FP8X4),
                 scales=w_scales[:, n * C : (n + 1) * C],
-                in_=w_grouped[:].rearrange("p o t -> p (o t)"),
+                in_=w_grouped[n][:].rearrange("p o t -> p (o t)"),
             )
 
-        moments = {}
+        means = {}
+        stds = {}
+        inverse = {}
         normed = {}
+        banks = {}
         chunks = {}
+        grouped = {}
         quantised = {}
 
-        def statistics(g):
+        def statistics_on_vector(g):
             stats = small.tile([P, GROUP, 6], F32)
             for j in range(GROUP):
                 nc.vector.bn_stats(out=stats[:, j, :], in_=x_tiles[g][:, j, :])
             mean_var = small.tile([P, GROUP, 2], F32)
             for j in range(GROUP):
                 nc.vector.bn_aggr(out=mean_var[:, j, :], in_=stats[:, j, :])
-            std = small.tile([P, GROUP], F32)
-            nc.scalar.activation(out=std[:], in_=mean_var[:, :, 1], func=ACT.Sqrt, bias=eps[:, 0:1], scale=1.0)
-            rstd = small.tile([P, GROUP], F32)
-            nc.vector.reciprocal(out=rstd[:], in_=std[:])
-            shift = small.tile([P, GROUP], F32)
-            nc.vector.scalar_tensor_tensor(
-                out=shift[:], in0=mean_var[:, :, 0], scalar=-1.0, in1=rstd[:], op0=ALU.mult, op1=ALU.mult
-            )
-            moments[g] = (rstd, shift)
+            means[g] = [mean_var[:, j, 0:1] for j in range(GROUP)]
+            stds[g] = small.tile([P, GROUP], F32, name="std")
+            nc.scalar.activation(out=stds[g][:], in_=mean_var[:, :, 1], func=ACT.Sqrt, bias=eps[:, 0:1], scale=1.0)
 
-        def normalise(g):
-            rstd, shift = moments[g]
-            xn = work.tile([P, GROUP, C], F32)
+        def statistics_on_scalar(g):
+            unread = work.tile([P, 2 * GROUP, C], BF16, bufs=1)
+            sums = small.tile([P, GROUP], F32)
             for j in range(GROUP):
                 nc.scalar.activation(
-                    out=xn[:, j, :],
-                    in_=x_tiles[g][:, j, :],
-                    func=ACT.Identity,
-                    scale=rstd[:, j : j + 1],
-                    bias=shift[:, j : j + 1],
+                    out=unread[:, j, :], in_=x_tiles[g][:, j, :], func=ACT.Identity, accum_out=sums[:, j : j + 1]
                 )
-            normed[g] = xn
+            mean = small.tile([P, GROUP], F32)
+            nc.scalar.mul(out=mean[:], in_=sums[:], mul=1.0 / C)
+            squares = small.tile([P, GROUP], F32)
+            for j in range(GROUP):
+                nc.scalar.activation(
+                    out=unread[:, GROUP + j, :],
+                    in_=x_tiles[g][:, j, :],
+                    func=ACT.Square,
+                    scale=-1.0,
+                    bias=mean[:, j : j + 1],
+                    accum_out=squares[:, j : j + 1],
+                )
+            means[g] = [mean[:, j : j + 1] for j in range(GROUP)]
+            stds[g] = small.tile([P, GROUP], F32, name="std")
+            nc.scalar.activation(out=stds[g][:], in_=squares[:], func=ACT.Sqrt, bias=eps[:, 0:1], scale=1.0 / C)
 
-        def transpose_and_scale(g):
+        def invert_std(g):
+            inverse[g] = small.tile([P, GROUP], F32, name="rstd")
+            nc.vector.reciprocal(out=inverse[g][:], in_=stds[g][:])
+
+        def normalise(g):
+            normed[g] = work.tile([P, GROUP, C], F32, name="xn")
+            for j in range(GROUP):
+                nc.gpsimd.tensor_scalar(
+                    out=normed[g][:, j, :],
+                    in0=x_tiles[g][:, j, :],
+                    scalar1=means[g][j],
+                    scalar2=inverse[g][:, j : j + 1],
+                    op0=ALU.subtract,
+                    op1=ALU.mult,
+                )
+
+        def transposes(g):
             half = g % HALVES
-            h_chunks = work.tile([P, PACK, GROUP * P], BF16)
+            banks[g] = []
             for t in range(PACK):
                 xt = psum_t.tile([P, GROUP, P], F32, tag="xt")
                 for j in range(GROUP):
                     nc.tensor.transpose(xt[:, j, :], normed[g][:, j, t * P : (t + 1) * P], perm[:, half, :])
+                banks[g].append(xt)
+
+        def gain_and_bias(g):
+            chunks[g] = work.tile([P, PACK, GROUP * P], BF16, name="h_chunks")
+            for t in range(PACK):
                 nc.scalar.activation(
-                    out=h_chunks[:, t, :],
-                    in_=xt[:].rearrange("p j m -> p (j m)"),
+                    out=chunks[g][:, t, :],
+                    in_=banks[g][t][:].rearrange("p j m -> p (j m)"),
                     func=ACT.Identity,
                     scale=norm_cols[:, t : t + 1],
                     bias=norm_cols[:, PACK + t : PACK + t + 1],
                 )
-            chunks[g] = h_chunks
 
-        def group_and_quantise(g):
-            h_grouped = work.tile([P, GROUP * P, PACK], BF16, align_bytes=64)
-            nc.scalar.copy(
-                out=h_grouped[:].rearrange("p (m i) t -> p m t i", i=4),
-                in_=chunks[g][:].rearrange("p t (m i) -> p m t i", i=4),
+        def regroup(g):
+            grouped[g] = work.tile([P, GROUP * P, PACK], BF16, align_bytes=64, name="h_grouped")
+            nc.gpsimd.tensor_scalar(
+                out=grouped[g][:],
+                in0=chunks[g][:].rearrange("p t m -> p m t"),
+                scalar1=1.0,
+                scalar2=0.0,
+                op0=ALU.mult,
+                op1=ALU.add,
             )
+
+        def quantise(g):
             codes = work.tile([P, GROUP * P], U32, align_bytes=64)
             scales = work.tile([P, GROUP * P], U8, align_bytes=64)
-            nc.vector.quantize_mx(
-                out=codes[:].bitcast(FP8X4), scales=scales[:], in_=h_grouped[:].rearrange("p m t -> p (m t)")
-            )
+            width = GROUP * P // 2
+            for first in range(0, GROUP * P, width):
+                nc.vector.quantize_mx(
+                    out=codes[:, first : first + width].bitcast(FP8X4),
+                    scales=scales[:, first : first + width],
+                    in_=grouped[g][:, first : first + width, :].rearrange("p m t -> p (m t)"),
+                )
             quantised[g] = (codes, scales)
 
         def project(g):
@@ -231,21 +270,40 @@ def tile_swintransformerblock_pa_t_kernel(
                         out=out_views[n][batch][:, place0 : place0 + STORE_TILES, :], in_=results[n][:]
                     )
 
-        statistics(0)
+        statistics_on_vector(0)
+        invert_std(0)
         normalise(0)
-        for n in range(N_OUT):
-            quantise_weights(n)
-        transpose_and_scale(0)
-        statistics(1)
-        group_and_quantise(0)
+        transpose_weights(0)
+        transpose_weights(1)
+        statistics_on_vector(1)
+        invert_std(1)
+        transposes(0)
+        gain_and_bias(0)
         normalise(1)
-        for g in range(GROUPS):
-            project(g)
-            if g + 1 < GROUPS:
-                transpose_and_scale(g + 1)
-            if g + 2 < GROUPS:
-                statistics(g + 2)
-            if g + 1 < GROUPS:
-                group_and_quantise(g + 1)
-            if g + 2 < GROUPS:
-                normalise(g + 2)
+        quantise_weights(0)
+        quantise_weights(1)
+        transpose_weights(2)
+        statistics_on_vector(2)
+        invert_std(2)
+        regroup(0)
+        quantise_weights(2)
+        transposes(1)
+        quantise(0)
+        statistics_on_vector(3)
+
+        for s in range(GROUPS):
+            if s + 1 < GROUPS:
+                gain_and_bias(s + 1)
+            if s + 2 < GROUPS:
+                normalise(s + 2)
+            if s + 1 < GROUPS:
+                regroup(s + 1)
+            project(s)
+            if s + 1 < GROUPS:
+                quantise(s + 1)
+            if s + AHEAD - 1 < GROUPS:
+                invert_std(s + AHEAD - 1)
+            if s + AHEAD < GROUPS:
+                statistics_on_scalar(s + AHEAD)
+            if s + 2 < GROUPS:
+                transposes(s + 2)

@@ -152,7 +152,7 @@ def tile_swintransformerblock_pa_t_kernel(
             mean_var = small.tile([P, GROUP, 2], F32)
             for j in range(GROUP):
                 nc.vector.bn_aggr(out=mean_var[:, j, :], in_=stats[:, j, :])
-            means[g] = [mean_var[:, j, 0:1] for j in range(GROUP)]
+            means[g] = mean_var[:, :, 0]
             stds[g] = small.tile([P, GROUP], F32, name="std")
             nc.scalar.activation(out=stds[g][:], in_=mean_var[:, :, 1], func=ACT.Sqrt, bias=eps[:, 0:1], scale=1.0)
 
@@ -175,24 +175,30 @@ def tile_swintransformerblock_pa_t_kernel(
                     bias=mean[:, j : j + 1],
                     accum_out=squares[:, j : j + 1],
                 )
-            means[g] = [mean[:, j : j + 1] for j in range(GROUP)]
+            means[g] = mean[:]
             stds[g] = small.tile([P, GROUP], F32, name="std")
             nc.scalar.activation(out=stds[g][:], in_=squares[:], func=ACT.Sqrt, bias=eps[:, 0:1], scale=1.0 / C)
 
         def invert_std(g):
-            inverse[g] = small.tile([P, GROUP], F32, name="rstd")
-            nc.vector.reciprocal(out=inverse[g][:], in_=stds[g][:])
+            rstd = small.tile([P, GROUP], F32)
+            nc.vector.reciprocal(out=rstd[:], in_=stds[g][:])
+            shift = small.tile([P, GROUP], F32)
+            nc.vector.scalar_tensor_tensor(
+                out=shift[:], in0=means[g], scalar=-1.0, in1=rstd[:], op0=ALU.mult, op1=ALU.mult
+            )
+            inverse[g] = (rstd, shift)
 
         def normalise(g):
+            rstd, shift = inverse[g]
             normed[g] = work.tile([P, GROUP, C], F32, name="xn")
             for j in range(GROUP):
                 nc.gpsimd.tensor_scalar(
                     out=normed[g][:, j, :],
                     in0=x_tiles[g][:, j, :],
-                    scalar1=means[g][j],
-                    scalar2=inverse[g][:, j : j + 1],
-                    op0=ALU.subtract,
-                    op1=ALU.mult,
+                    scalar1=rstd[:, j : j + 1],
+                    scalar2=shift[:, j : j + 1],
+                    op0=ALU.mult,
+                    op1=ALU.add,
                 )
 
         def transposes(g):

@@ -27,6 +27,7 @@ ROW_TILES = C // P
 EPS = 1e-5
 OUT_SCALE = (64.0**-0.5, 1.0, 1.0)
 AHEAD = 4
+STORE_BUFFERS = 12
 
 FLOPS = 2 * BATCHES * GRID * GRID * C * N_OUT * C
 
@@ -47,7 +48,7 @@ def tile_swintransformerblock_pa_t_kernel(
         tc.tile_pool(name="const", bufs=1) as const,
         tc.tile_pool(name="small", bufs=AHEAD) as small,
         tc.tile_pool(name="work", bufs=2) as work,
-        tc.tile_pool(name="stage", bufs=4) as stage,
+        tc.tile_pool(name="stage", bufs=STORE_BUFFERS) as stage,
         tc.psum_pool(name="psum_t", bufs=4) as psum_t,
         tc.psum_pool(name="psum_acc", bufs=4) as psum_acc,
         tc.manual_schedule(),
@@ -100,16 +101,22 @@ def tile_swintransformerblock_pa_t_kernel(
         nc.vector.tensor_copy(out=perm_1[:, :, 0 : WINDOWS - 1, :], in_=rolled_v[:, :, 1:WINDOWS, :])
         nc.vector.tensor_copy(out=perm_1[:, :, WINDOWS - 1 : WINDOWS, :], in_=rolled_v[:, :, 0:1, :])
 
-        norm_cols_ps = psum_t.tile([P, P], BF16, tag="xt")
-        nc.tensor.transpose(norm_cols_ps[:], norm_rows[:], ident_bf16[:])
         norm_cols = const.tile([P, 2 * PACK], F32)
-        nc.vector.tensor_copy(out=norm_cols[:], in_=norm_cols_ps[:, 0 : 2 * PACK])
+
+        def spread_gain_and_bias():
+            norm_cols_ps = psum_t.tile([P, P], BF16, tag="xt")
+            nc.tensor.transpose(norm_cols_ps[:], norm_rows[:], ident_bf16[:])
+            nc.vector.tensor_copy(out=norm_cols[:], in_=norm_cols_ps[:, 0 : 2 * PACK])
 
         bias_all = const.tile([P, N_OUT, C], F32)
-        for n in range(N_OUT):
-            bias_ps = psum_acc.tile([P, C], F32, tag="acc")
-            nc.tensor.matmul(bias_ps[:], lhsT=ones[:], rhs=bias_row[:, n * C : (n + 1) * C], start=True, stop=True)
-            nc.scalar.activation(out=bias_all[:, n, :], in_=bias_ps[:], func=ACT.Copy, scale=OUT_SCALE[n])
+
+        def spread_projection_bias():
+            for n in range(N_OUT):
+                bias_ps = psum_acc.tile([P, C], F32, tag="acc")
+                nc.tensor.matmul(
+                    bias_ps[:], lhsT=ones[:], rhs=bias_row[:, n * C : (n + 1) * C], start=True, stop=True
+                )
+                nc.scalar.activation(out=bias_all[:, n, :], in_=bias_ps[:], func=ACT.Copy, scale=OUT_SCALE[n])
 
         w_codes = const.tile([P, N_OUT * C], U32, align_bytes=64)
         w_scales = const.tile([P, N_OUT * C], U8, align_bytes=64)
@@ -248,10 +255,11 @@ def tile_swintransformerblock_pa_t_kernel(
             batch, half = divmod(g, HALVES)
             codes, scales = quantised[g]
             for first in range(0, GROUP, STORE_TILES):
-                results = [stage.tile([P, STORE_TILES, C], F32, name="result_%d" % n) for n in range(N_OUT)]
-                for i in range(STORE_TILES):
-                    j = first + i
-                    for n in range(N_OUT):
+                place0 = GROUP * half + first
+                for n in range(N_OUT):
+                    result = stage.tile([P, STORE_TILES, C], F32)
+                    for i in range(STORE_TILES):
+                        j = first + i
                         acc = psum_acc.tile([P, C], F32, tag="acc")
                         nc.tensor.matmul_mx(
                             out=acc[:],
@@ -263,39 +271,37 @@ def tile_swintransformerblock_pa_t_kernel(
                             stop=True,
                         )
                         nc.vector.scalar_tensor_tensor(
-                            out=results[n][:, i, :],
+                            out=result[:, i, :],
                             in0=acc[:],
                             scalar=OUT_SCALE[n],
                             in1=bias_all[:, n, :],
                             op0=ALU.mult,
                             op1=ALU.add,
                         )
-                place0 = GROUP * half + first
-                for n in range(N_OUT):
-                    nc.sync.dma_start(
-                        out=out_views[n][batch][:, place0 : place0 + STORE_TILES, :], in_=results[n][:]
-                    )
+                    nc.sync.dma_start(out=out_views[n][batch][:, place0 : place0 + STORE_TILES, :], in_=result[:])
 
         statistics_on_vector(0)
         invert_std(0)
         normalise(0)
         transpose_weights(0)
-        transpose_weights(1)
         statistics_on_vector(1)
         invert_std(1)
+        transpose_weights(1)
+        spread_gain_and_bias()
         transposes(0)
         gain_and_bias(0)
         normalise(1)
+        statistics_on_vector(2)
         quantise_weights(0)
         quantise_weights(1)
-        transpose_weights(2)
-        statistics_on_vector(2)
         invert_std(2)
+        transpose_weights(2)
+        statistics_on_vector(3)
         regroup(0)
         quantise_weights(2)
         transposes(1)
+        spread_projection_bias()
         quantise(0)
-        statistics_on_vector(3)
 
         for s in range(GROUPS):
             if s + 1 < GROUPS:

@@ -13,21 +13,25 @@ P = 128
 PACK = 4
 C = P * PACK
 BATCHES = 4
-SLOTS = 8
-GROUP = 4
-HALVES = SLOTS // GROUP
-GROUPS = BATCHES * HALVES
-STORE_TILES = 2
 GRID = 32
 WINDOW = 8
 SHIFT = 4
 WINDOWS = GRID // WINDOW
+SLOTS = WINDOW
+GROUP = 4
+HALVES = SLOTS // GROUP
+GROUPS = BATCHES * HALVES
 N_OUT = 3
-ROW_TILES = C // P
-EPS = 1e-5
 OUT_SCALE = (64.0**-0.5, 1.0, 1.0)
+ROW_TILES = C // P
+TILES_PER_BANK = 2
+EPS = 1e-5
+BN_STATS_DIM = 6
+BN_AGGR_DIM = 2
 AHEAD = 4
+STORE_TILES = 2
 STORE_BUFFERS = 12
+ACC_BANKS = 4
 
 FLOPS = 2 * BATCHES * GRID * GRID * C * N_OUT * C
 
@@ -48,9 +52,9 @@ def tile_swintransformerblock_pa_t_kernel(
         tc.tile_pool(name="const", bufs=1) as const,
         tc.tile_pool(name="small", bufs=AHEAD) as small,
         tc.tile_pool(name="work", bufs=2) as work,
-        tc.tile_pool(name="stage", bufs=STORE_BUFFERS) as stage,
-        tc.psum_pool(name="psum_t", bufs=4) as psum_t,
-        tc.psum_pool(name="psum_acc", bufs=4) as psum_acc,
+        tc.tile_pool(name="results", bufs=STORE_BUFFERS) as results,
+        tc.psum_pool(name="psum_t", bufs=PACK) as psum_t,
+        tc.psum_pool(name="psum_acc", bufs=ACC_BANKS) as psum_acc,
         tc.manual_schedule(),
     ):
         x_tiles = [const.tile([P, GROUP, C], BF16, name="x_%d" % g) for g in range(GROUPS)]
@@ -76,9 +80,9 @@ def tile_swintransformerblock_pa_t_kernel(
         nc.vector.memset(norm_rows[:], 0.0)
         nc.scalar.dma_start(out=norm_rows[0:PACK, :], in_=ln1_w.rearrange("(t p) -> t p", p=P))
         nc.scalar.dma_start(out=norm_rows[PACK : 2 * PACK, :], in_=ln1_b.rearrange("(t p) -> t p", p=P))
-        bias_row = const.tile([P, N_OUT * C], BF16)
-        nc.vector.memset(bias_row[:], 0.0)
-        nc.scalar.dma_start(out=bias_row[0:1, :], in_=in_proj_b.rearrange("(o n) -> o n", o=1))
+        proj_bias_row = const.tile([P, N_OUT * C], BF16)
+        nc.vector.memset(proj_bias_row[:], 0.0)
+        nc.scalar.dma_start(out=proj_bias_row[0:1, :], in_=in_proj_b.rearrange("(o n) -> o n", o=1))
 
         ident_f32 = const.tile([P, P], F32)
         make_identity(nc, ident_f32[:])
@@ -103,36 +107,39 @@ def tile_swintransformerblock_pa_t_kernel(
 
         norm_cols = const.tile([P, 2 * PACK], F32)
 
-        def spread_gain_and_bias():
+        def spread_norm_vectors():
             norm_cols_ps = psum_t.tile([P, P], BF16, tag="xt")
             nc.tensor.transpose(norm_cols_ps[:], norm_rows[:], ident_bf16[:])
             nc.vector.tensor_copy(out=norm_cols[:], in_=norm_cols_ps[:, 0 : 2 * PACK])
 
-        bias_all = const.tile([P, N_OUT, C], F32)
+        proj_bias = const.tile([P, N_OUT, C], F32)
 
-        def spread_projection_bias():
+        def spread_proj_bias():
             for n in range(N_OUT):
-                bias_ps = psum_acc.tile([P, C], F32, tag="acc")
+                proj_bias_ps = psum_acc.tile([P, C], F32, tag="acc")
                 nc.tensor.matmul(
-                    bias_ps[:], lhsT=ones[:], rhs=bias_row[:, n * C : (n + 1) * C], start=True, stop=True
+                    proj_bias_ps[:], lhsT=ones[:], rhs=proj_bias_row[:, n * C : (n + 1) * C], start=True, stop=True
                 )
-                nc.scalar.activation(out=bias_all[:, n, :], in_=bias_ps[:], func=ACT.Copy, scale=OUT_SCALE[n])
+                nc.scalar.activation(out=proj_bias[:, n, :], in_=proj_bias_ps[:], func=ACT.Copy, scale=OUT_SCALE[n])
 
         w_codes = const.tile([P, N_OUT * C], U32, align_bytes=64)
         w_scales = const.tile([P, N_OUT * C], U8, align_bytes=64)
-        w_grouped = {}
+        w_interleaved = {}
 
         def transpose_weights(n):
-            w_grouped[n] = work.tile([P, C, PACK], BF16, align_bytes=64, name="w_grouped")
-            for pair in range(ROW_TILES // 2):
-                wt = psum_acc.tile([P, 2, PACK, P], BF16, tag="acc")
-                for a in range(2):
+            w_interleaved[n] = work.tile([P, C, PACK], BF16, align_bytes=64, name="w_interleaved")
+            for bank in range(ROW_TILES // TILES_PER_BANK):
+                wt = psum_acc.tile([P, TILES_PER_BANK, PACK, P], BF16, tag="acc")
+                for a in range(TILES_PER_BANK):
                     for t in range(PACK):
                         nc.tensor.transpose(
-                            wt[:, a, t, :], w_raw[n][:, 2 * pair + a, t * P : (t + 1) * P], ident_bf16[:]
+                            wt[:, a, t, :], w_raw[n][:, TILES_PER_BANK * bank + a, t * P : (t + 1) * P], ident_bf16[:]
                         )
+                rows = TILES_PER_BANK * P
                 nc.scalar.copy(
-                    out=w_grouped[n][:, 2 * pair * P : 2 * (pair + 1) * P, :].rearrange("p (a o) t -> p a o t", a=2),
+                    out=w_interleaved[n][:, bank * rows : (bank + 1) * rows, :].rearrange(
+                        "p (a o) t -> p a o t", a=TILES_PER_BANK
+                    ),
                     in_=wt[:].rearrange("p a t o -> p a o t"),
                 )
 
@@ -140,23 +147,23 @@ def tile_swintransformerblock_pa_t_kernel(
             nc.vector.quantize_mx(
                 out=w_codes[:, n * C : (n + 1) * C].bitcast(FP8X4),
                 scales=w_scales[:, n * C : (n + 1) * C],
-                in_=w_grouped[n][:].rearrange("p o t -> p (o t)"),
+                in_=w_interleaved[n][:].rearrange("p o t -> p (o t)"),
             )
 
         means = {}
         stds = {}
-        inverse = {}
+        factors = {}
         normed = {}
         banks = {}
         chunks = {}
-        grouped = {}
+        interleaved = {}
         quantised = {}
 
         def statistics_on_vector(g):
-            stats = small.tile([P, GROUP, 6], F32)
+            stats = small.tile([P, GROUP, BN_STATS_DIM], F32)
             for j in range(GROUP):
                 nc.vector.bn_stats(out=stats[:, j, :], in_=x_tiles[g][:, j, :])
-            mean_var = small.tile([P, GROUP, 2], F32)
+            mean_var = small.tile([P, GROUP, BN_AGGR_DIM], F32)
             for j in range(GROUP):
                 nc.vector.bn_aggr(out=mean_var[:, j, :], in_=stats[:, j, :])
             means[g] = mean_var[:, :, 0]
@@ -189,21 +196,21 @@ def tile_swintransformerblock_pa_t_kernel(
         def invert_std(g):
             rstd = small.tile([P, GROUP], F32)
             nc.vector.reciprocal(out=rstd[:], in_=stds[g][:])
-            shift = small.tile([P, GROUP], F32)
+            offset = small.tile([P, GROUP], F32)
             nc.vector.scalar_tensor_tensor(
-                out=shift[:], in0=means[g], scalar=-1.0, in1=rstd[:], op0=ALU.mult, op1=ALU.mult
+                out=offset[:], in0=means[g], scalar=-1.0, in1=rstd[:], op0=ALU.mult, op1=ALU.mult
             )
-            inverse[g] = (rstd, shift)
+            factors[g] = (rstd, offset)
 
         def normalise(g):
-            rstd, shift = inverse[g]
+            rstd, offset = factors[g]
             normed[g] = work.tile([P, GROUP, C], F32, name="xn")
             for j in range(GROUP):
                 nc.gpsimd.tensor_scalar(
                     out=normed[g][:, j, :],
                     in0=x_tiles[g][:, j, :],
                     scalar1=rstd[:, j : j + 1],
-                    scalar2=shift[:, j : j + 1],
+                    scalar2=offset[:, j : j + 1],
                     op0=ALU.mult,
                     op1=ALU.add,
                 )
@@ -228,10 +235,10 @@ def tile_swintransformerblock_pa_t_kernel(
                     bias=norm_cols[:, PACK + t : PACK + t + 1],
                 )
 
-        def regroup(g):
-            grouped[g] = work.tile([P, GROUP * P, PACK], BF16, align_bytes=64, name="h_grouped")
+        def interleave(g):
+            interleaved[g] = work.tile([P, GROUP * P, PACK], BF16, align_bytes=64, name="h_interleaved")
             nc.gpsimd.tensor_scalar(
-                out=grouped[g][:],
+                out=interleaved[g][:],
                 in0=chunks[g][:].rearrange("p t m -> p m t"),
                 scalar1=1.0,
                 scalar2=0.0,
@@ -243,23 +250,23 @@ def tile_swintransformerblock_pa_t_kernel(
             codes = work.tile([P, GROUP * P], U32, align_bytes=64)
             scales = work.tile([P, GROUP * P], U8, align_bytes=64)
             width = GROUP * P // 2
-            for first in range(0, GROUP * P, width):
+            for col0 in range(0, GROUP * P, width):
                 nc.vector.quantize_mx(
-                    out=codes[:, first : first + width].bitcast(FP8X4),
-                    scales=scales[:, first : first + width],
-                    in_=grouped[g][:, first : first + width, :].rearrange("p m t -> p (m t)"),
+                    out=codes[:, col0 : col0 + width].bitcast(FP8X4),
+                    scales=scales[:, col0 : col0 + width],
+                    in_=interleaved[g][:, col0 : col0 + width, :].rearrange("p m t -> p (m t)"),
                 )
             quantised[g] = (codes, scales)
 
         def project(g):
             batch, half = divmod(g, HALVES)
             codes, scales = quantised[g]
-            for first in range(0, GROUP, STORE_TILES):
-                place0 = GROUP * half + first
+            for tile0 in range(0, GROUP, STORE_TILES):
+                place0 = GROUP * half + tile0
                 for n in range(N_OUT):
-                    result = stage.tile([P, STORE_TILES, C], F32)
+                    result = results.tile([P, STORE_TILES, C], F32)
                     for i in range(STORE_TILES):
-                        j = first + i
+                        j = tile0 + i
                         acc = psum_acc.tile([P, C], F32, tag="acc")
                         nc.tensor.matmul_mx(
                             out=acc[:],
@@ -274,7 +281,7 @@ def tile_swintransformerblock_pa_t_kernel(
                             out=result[:, i, :],
                             in0=acc[:],
                             scalar=OUT_SCALE[n],
-                            in1=bias_all[:, n, :],
+                            in1=proj_bias[:, n, :],
                             op0=ALU.mult,
                             op1=ALU.add,
                         )
@@ -287,7 +294,7 @@ def tile_swintransformerblock_pa_t_kernel(
         statistics_on_vector(1)
         invert_std(1)
         transpose_weights(1)
-        spread_gain_and_bias()
+        spread_norm_vectors()
         transposes(0)
         gain_and_bias(0)
         normalise(1)
@@ -297,10 +304,10 @@ def tile_swintransformerblock_pa_t_kernel(
         invert_std(2)
         transpose_weights(2)
         statistics_on_vector(3)
-        regroup(0)
+        interleave(0)
         quantise_weights(2)
         transposes(1)
-        spread_projection_bias()
+        spread_proj_bias()
         quantise(0)
 
         for s in range(GROUPS):
@@ -309,7 +316,7 @@ def tile_swintransformerblock_pa_t_kernel(
             if s + 2 < GROUPS:
                 normalise(s + 2)
             if s + 1 < GROUPS:
-                regroup(s + 1)
+                interleave(s + 1)
             project(s)
             if s + 1 < GROUPS:
                 quantise(s + 1)

@@ -32,6 +32,8 @@ AHEAD = 4
 STORE_TILES = 2
 STORE_BUFFERS = 12
 ACC_BANKS = 4
+HALF_COLS = GROUP * P // 2
+QUANTISE_AHEAD = (3, 1)
 
 FLOPS = 2 * BATCHES * GRID * GRID * C * N_OUT * C
 
@@ -92,6 +94,8 @@ def tile_swintransformerblock_pa_t_kernel(
         nc.vector.memset(ones[:], 1.0)
         eps = const.tile([P, 1], F32)
         nc.vector.memset(eps[:], EPS)
+        table_warmer = const.tile([P, 1], F32)
+        nc.scalar.activation(out=table_warmer[:], in_=eps[:], func=ACT.Abs_reciprocal_sqrt)
 
         rolled = const.tile([P, P], F32)
         turn = SHIFT * WINDOWS
@@ -150,9 +154,9 @@ def tile_swintransformerblock_pa_t_kernel(
                 in_=w_interleaved[n][:].rearrange("p o t -> p (o t)"),
             )
 
-        means = {}
-        stds = {}
-        factors = {}
+        negative_means = {}
+        rstds = {}
+        offsets = {}
         normed = {}
         banks = {}
         chunks = {}
@@ -166,51 +170,55 @@ def tile_swintransformerblock_pa_t_kernel(
             mean_var = small.tile([P, GROUP, BN_AGGR_DIM], F32)
             for j in range(GROUP):
                 nc.vector.bn_aggr(out=mean_var[:, j, :], in_=stats[:, j, :])
-            means[g] = mean_var[:, :, 0]
-            stds[g] = small.tile([P, GROUP], F32, name="std")
-            nc.scalar.activation(out=stds[g][:], in_=mean_var[:, :, 1], func=ACT.Sqrt, bias=eps[:, 0:1], scale=1.0)
+            negative_mean = small.tile([P, GROUP], F32)
+            nc.vector.tensor_scalar(
+                out=negative_mean[:], in0=mean_var[:, :, 0], scalar1=-1.0, scalar2=0.0, op0=ALU.mult, op1=ALU.add
+            )
+            negative_means[g] = negative_mean
+            rstds[g] = small.tile([P, GROUP], F32, name="rstd")
+            nc.scalar.activation(
+                out=rstds[g][:], in_=mean_var[:, :, 1], func=ACT.Abs_reciprocal_sqrt, bias=eps[:, 0:1], scale=1.0
+            )
 
         def statistics_on_scalar(g):
             unread = work.tile([P, 2 * GROUP, C], BF16, bufs=1)
-            sums = small.tile([P, GROUP], F32)
+            negative_mean = small.tile([P, GROUP], F32)
             for j in range(GROUP):
                 nc.scalar.activation(
-                    out=unread[:, j, :], in_=x_tiles[g][:, j, :], func=ACT.Identity, accum_out=sums[:, j : j + 1]
+                    out=unread[:, j, :],
+                    in_=x_tiles[g][:, j, :],
+                    func=ACT.Identity,
+                    scale=-1.0 / C,
+                    accum_out=negative_mean[:, j : j + 1],
                 )
-            mean = small.tile([P, GROUP], F32)
-            nc.scalar.mul(out=mean[:], in_=sums[:], mul=1.0 / C)
             squares = small.tile([P, GROUP], F32)
             for j in range(GROUP):
                 nc.scalar.activation(
                     out=unread[:, GROUP + j, :],
                     in_=x_tiles[g][:, j, :],
                     func=ACT.Square,
-                    scale=-1.0,
-                    bias=mean[:, j : j + 1],
+                    scale=1.0,
+                    bias=negative_mean[:, j : j + 1],
                     accum_out=squares[:, j : j + 1],
                 )
-            means[g] = mean[:]
-            stds[g] = small.tile([P, GROUP], F32, name="std")
-            nc.scalar.activation(out=stds[g][:], in_=squares[:], func=ACT.Sqrt, bias=eps[:, 0:1], scale=1.0 / C)
-
-        def invert_std(g):
-            rstd = small.tile([P, GROUP], F32)
-            nc.vector.reciprocal(out=rstd[:], in_=stds[g][:])
-            offset = small.tile([P, GROUP], F32)
-            nc.vector.scalar_tensor_tensor(
-                out=offset[:], in0=means[g], scalar=-1.0, in1=rstd[:], op0=ALU.mult, op1=ALU.mult
+            negative_means[g] = negative_mean
+            rstds[g] = small.tile([P, GROUP], F32, name="rstd")
+            nc.scalar.activation(
+                out=rstds[g][:], in_=squares[:], func=ACT.Abs_reciprocal_sqrt, bias=eps[:, 0:1], scale=1.0 / C
             )
-            factors[g] = (rstd, offset)
+
+        def offset(g):
+            offsets[g] = small.tile([P, GROUP], F32, name="offset")
+            nc.gpsimd.tensor_tensor(out=offsets[g][:], in0=negative_means[g][:], in1=rstds[g][:], op=ALU.mult)
 
         def normalise(g):
-            rstd, offset = factors[g]
             normed[g] = work.tile([P, GROUP, C], F32, name="xn")
             for j in range(GROUP):
                 nc.gpsimd.tensor_scalar(
                     out=normed[g][:, j, :],
                     in0=x_tiles[g][:, j, :],
-                    scalar1=rstd[:, j : j + 1],
-                    scalar2=offset[:, j : j + 1],
+                    scalar1=rstds[g][:, j : j + 1],
+                    scalar2=offsets[g][:, j : j + 1],
                     op0=ALU.mult,
                     op1=ALU.add,
                 )
@@ -237,36 +245,42 @@ def tile_swintransformerblock_pa_t_kernel(
 
         def interleave(g):
             interleaved[g] = work.tile([P, GROUP * P, PACK], BF16, align_bytes=64, name="h_interleaved")
-            nc.gpsimd.tensor_scalar(
-                out=interleaved[g][:],
-                in0=chunks[g][:].rearrange("p t m -> p m t"),
-                scalar1=1.0,
-                scalar2=0.0,
-                op0=ALU.mult,
-                op1=ALU.add,
-            )
-
-        def quantise(g):
-            codes = work.tile([P, GROUP * P], U32, align_bytes=64)
-            scales = work.tile([P, GROUP * P], U8, align_bytes=64)
-            width = GROUP * P // 2
-            for col0 in range(0, GROUP * P, width):
-                nc.vector.quantize_mx(
-                    out=codes[:, col0 : col0 + width].bitcast(FP8X4),
-                    scales=scales[:, col0 : col0 + width],
-                    in_=interleaved[g][:, col0 : col0 + width, :].rearrange("p m t -> p (m t)"),
+            for col0 in range(0, GROUP * P, HALF_COLS):
+                nc.gpsimd.tensor_scalar(
+                    out=interleaved[g][:, col0 : col0 + HALF_COLS, :],
+                    in0=chunks[g][:, :, col0 : col0 + HALF_COLS].rearrange("p t m -> p m t"),
+                    scalar1=1.0,
+                    scalar2=0.0,
+                    op0=ALU.mult,
+                    op1=ALU.add,
                 )
-            quantised[g] = (codes, scales)
+
+        def quantise(g, part):
+            if part == 0:
+                codes = work.tile([P, GROUP * P], U32, align_bytes=64)
+                scales = work.tile([P, GROUP * P], U8, align_bytes=64)
+                quantised[g] = (codes, scales)
+            codes, scales = quantised[g]
+            col0 = part * HALF_COLS
+            nc.vector.quantize_mx(
+                out=codes[:, col0 : col0 + HALF_COLS].bitcast(FP8X4),
+                scales=scales[:, col0 : col0 + HALF_COLS],
+                in_=interleaved[g][:, col0 : col0 + HALF_COLS, :].rearrange("p m t -> p (m t)"),
+            )
 
         def project(g):
             batch, half = divmod(g, HALVES)
             codes, scales = quantised[g]
+            left = GROUP * N_OUT
             for tile0 in range(0, GROUP, STORE_TILES):
                 place0 = GROUP * half + tile0
                 for n in range(N_OUT):
                     result = results.tile([P, STORE_TILES, C], F32)
                     for i in range(STORE_TILES):
                         j = tile0 + i
+                        if g + 1 < GROUPS and left in QUANTISE_AHEAD:
+                            quantise(g + 1, QUANTISE_AHEAD.index(left))
+                        left -= 1
                         acc = psum_acc.tile([P, C], F32, tag="acc")
                         nc.tensor.matmul_mx(
                             out=acc[:],
@@ -288,11 +302,11 @@ def tile_swintransformerblock_pa_t_kernel(
                     nc.sync.dma_start(out=out_views[n][batch][:, place0 : place0 + STORE_TILES, :], in_=result[:])
 
         statistics_on_vector(0)
-        invert_std(0)
+        offset(0)
         normalise(0)
         transpose_weights(0)
         statistics_on_vector(1)
-        invert_std(1)
+        offset(1)
         transpose_weights(1)
         spread_norm_vectors()
         transposes(0)
@@ -301,14 +315,15 @@ def tile_swintransformerblock_pa_t_kernel(
         statistics_on_vector(2)
         quantise_weights(0)
         quantise_weights(1)
-        invert_std(2)
+        offset(2)
         transpose_weights(2)
         statistics_on_vector(3)
         interleave(0)
         quantise_weights(2)
         transposes(1)
         spread_proj_bias()
-        quantise(0)
+        quantise(0, 0)
+        quantise(0, 1)
 
         for s in range(GROUPS):
             if s + 1 < GROUPS:
@@ -318,10 +333,8 @@ def tile_swintransformerblock_pa_t_kernel(
             if s + 1 < GROUPS:
                 interleave(s + 1)
             project(s)
-            if s + 1 < GROUPS:
-                quantise(s + 1)
             if s + AHEAD - 1 < GROUPS:
-                invert_std(s + AHEAD - 1)
+                offset(s + AHEAD - 1)
             if s + AHEAD < GROUPS:
                 statistics_on_scalar(s + AHEAD)
             if s + 2 < GROUPS:

@@ -32,8 +32,7 @@ AHEAD = 4
 STORE_TILES = 2
 STORE_BUFFERS = 12
 ACC_BANKS = 4
-HALF_COLS = GROUP * P // 2
-QUANTISE_AHEAD = (3, 1)
+QUANTISE_AHEAD = 2
 
 FLOPS = 2 * BATCHES * GRID * GRID * C * N_OUT * C
 
@@ -209,7 +208,7 @@ def tile_swintransformerblock_pa_t_kernel(
 
         def offset(g):
             offsets[g] = small.tile([P, GROUP], F32, name="offset")
-            nc.gpsimd.tensor_tensor(out=offsets[g][:], in0=negative_means[g][:], in1=rstds[g][:], op=ALU.mult)
+            nc.vector.tensor_tensor(out=offsets[g][:], in0=negative_means[g][:], in1=rstds[g][:], op=ALU.mult)
 
         def normalise(g):
             normed[g] = work.tile([P, GROUP, C], F32, name="xn")
@@ -245,28 +244,22 @@ def tile_swintransformerblock_pa_t_kernel(
 
         def interleave(g):
             interleaved[g] = work.tile([P, GROUP * P, PACK], BF16, align_bytes=64, name="h_interleaved")
-            for col0 in range(0, GROUP * P, HALF_COLS):
-                nc.gpsimd.tensor_scalar(
-                    out=interleaved[g][:, col0 : col0 + HALF_COLS, :],
-                    in0=chunks[g][:, :, col0 : col0 + HALF_COLS].rearrange("p t m -> p m t"),
-                    scalar1=1.0,
-                    scalar2=0.0,
-                    op0=ALU.mult,
-                    op1=ALU.add,
-                )
-
-        def quantise(g, part):
-            if part == 0:
-                codes = work.tile([P, GROUP * P], U32, align_bytes=64)
-                scales = work.tile([P, GROUP * P], U8, align_bytes=64)
-                quantised[g] = (codes, scales)
-            codes, scales = quantised[g]
-            col0 = part * HALF_COLS
-            nc.vector.quantize_mx(
-                out=codes[:, col0 : col0 + HALF_COLS].bitcast(FP8X4),
-                scales=scales[:, col0 : col0 + HALF_COLS],
-                in_=interleaved[g][:, col0 : col0 + HALF_COLS, :].rearrange("p m t -> p (m t)"),
+            nc.gpsimd.tensor_scalar(
+                out=interleaved[g][:],
+                in0=chunks[g][:].rearrange("p t m -> p m t"),
+                scalar1=1.0,
+                scalar2=0.0,
+                op0=ALU.mult,
+                op1=ALU.add,
             )
+
+        def quantise(g):
+            codes = work.tile([P, GROUP * P], U32, align_bytes=64)
+            scales = work.tile([P, GROUP * P], U8, align_bytes=64)
+            nc.vector.quantize_mx(
+                out=codes[:].bitcast(FP8X4), scales=scales[:], in_=interleaved[g][:].rearrange("p m t -> p (m t)")
+            )
+            quantised[g] = (codes, scales)
 
         def project(g):
             batch, half = divmod(g, HALVES)
@@ -278,8 +271,11 @@ def tile_swintransformerblock_pa_t_kernel(
                     result = results.tile([P, STORE_TILES, C], F32)
                     for i in range(STORE_TILES):
                         j = tile0 + i
-                        if g + 1 < GROUPS and left in QUANTISE_AHEAD:
-                            quantise(g + 1, QUANTISE_AHEAD.index(left))
+                        if left == QUANTISE_AHEAD:
+                            if g + 1 < GROUPS:
+                                quantise(g + 1)
+                            if g + AHEAD - 1 < GROUPS:
+                                offset(g + AHEAD - 1)
                         left -= 1
                         acc = psum_acc.tile([P, C], F32, tag="acc")
                         nc.tensor.matmul_mx(
@@ -322,8 +318,7 @@ def tile_swintransformerblock_pa_t_kernel(
         quantise_weights(2)
         transposes(1)
         spread_proj_bias()
-        quantise(0, 0)
-        quantise(0, 1)
+        quantise(0)
 
         for s in range(GROUPS):
             if s + 1 < GROUPS:
@@ -333,8 +328,6 @@ def tile_swintransformerblock_pa_t_kernel(
             if s + 1 < GROUPS:
                 interleave(s + 1)
             project(s)
-            if s + AHEAD - 1 < GROUPS:
-                offset(s + AHEAD - 1)
             if s + AHEAD < GROUPS:
                 statistics_on_scalar(s + AHEAD)
             if s + 2 < GROUPS:

@@ -25,6 +25,7 @@ N_OUT = 3
 OUT_SCALE = (64.0**-0.5, 1.0, 1.0)
 ROW_TILES = C // P
 TILES_PER_BANK = 2
+BIAS_ROWS = N_OUT * C // P
 EPS = 1e-5
 BN_STATS_DIM = 6
 BN_AGGR_DIM = 2
@@ -61,36 +62,41 @@ def tile_swintransformerblock_pa_t_kernel(
         x_tiles = [const.tile([P, GROUP, C], BF16, name="x_%d" % g) for g in range(GROUPS)]
         w_raw = [const.tile([P, ROW_TILES, C], BF16, name="w_raw_%d" % n) for n in range(N_OUT)]
 
-        def load_x(g):
+        small_rows = const.tile([P, P], BF16)
+        nc.vector.memset(small_rows[:], 0.0)
+
+        def load_x(g, tile0, tiles):
             batch, half = divmod(g, HALVES)
-            slot0 = (SHIFT + GROUP * half) % SLOTS
-            nc.sync.dma_start(out=x_tiles[g][:], in_=x_view[batch][:, slot0 : slot0 + GROUP, :])
+            slot0 = (SHIFT + GROUP * half) % SLOTS + tile0
+            nc.sync.dma_start(
+                out=x_tiles[g][:, tile0 : tile0 + tiles, :], in_=x_view[batch][:, slot0 : slot0 + tiles, :]
+            )
 
         def load_w(n):
             nc.sync.dma_start(out=w_raw[n][:], in_=w_view[:, n * ROW_TILES : (n + 1) * ROW_TILES, :])
 
-        load_x(0)
+        load_x(0, 0, GROUP // 2)
+        nc.sync.dma_start(out=small_rows[0:PACK, :], in_=ln1_w.rearrange("(t p) -> t p", p=P))
+        nc.sync.dma_start(out=small_rows[PACK : 2 * PACK, :], in_=ln1_b.rearrange("(t p) -> t p", p=P))
+        nc.sync.dma_start(
+            out=small_rows[2 * PACK : 2 * PACK + BIAS_ROWS, :], in_=in_proj_b.rearrange("(r p) -> r p", p=P)
+        )
+        load_x(0, GROUP // 2, GROUP // 2)
         load_w(0)
-        load_x(1)
+        load_x(1, 0, GROUP)
         load_w(1)
         load_w(2)
         for g in range(2, GROUPS):
-            load_x(g)
-
-        norm_rows = const.tile([P, P], BF16)
-        nc.vector.memset(norm_rows[:], 0.0)
-        nc.scalar.dma_start(out=norm_rows[0:PACK, :], in_=ln1_w.rearrange("(t p) -> t p", p=P))
-        nc.scalar.dma_start(out=norm_rows[PACK : 2 * PACK, :], in_=ln1_b.rearrange("(t p) -> t p", p=P))
-        proj_bias_row = const.tile([P, N_OUT * C], BF16)
-        nc.vector.memset(proj_bias_row[:], 0.0)
-        nc.scalar.dma_start(out=proj_bias_row[0:1, :], in_=in_proj_b.rearrange("(o n) -> o n", o=1))
+            load_x(g, 0, GROUP)
 
         ident_f32 = const.tile([P, P], F32)
         make_identity(nc, ident_f32[:])
         ident_bf16 = const.tile([P, P], BF16)
         nc.vector.tensor_copy(out=ident_bf16[:], in_=ident_f32[:])
-        ones = const.tile([P, P], BF16)
-        nc.vector.memset(ones[:], 1.0)
+        ident_q = const.tile([P, P], BF16)
+        nc.vector.tensor_scalar(
+            out=ident_q[:], in0=ident_f32[:], scalar1=OUT_SCALE[0], scalar2=0.0, op0=ALU.mult, op1=ALU.add
+        )
         eps = const.tile([P, 1], F32)
         nc.vector.memset(eps[:], EPS)
         table_warmer = const.tile([P, 1], F32)
@@ -109,21 +115,29 @@ def tile_swintransformerblock_pa_t_kernel(
         nc.vector.tensor_copy(out=perm_1[:, :, WINDOWS - 1 : WINDOWS, :], in_=rolled_v[:, :, 0:1, :])
 
         norm_cols = const.tile([P, 2 * PACK], F32)
+        bias_cols = const.tile([P, BIAS_ROWS], BF16)
 
-        def spread_norm_vectors():
-            norm_cols_ps = psum_t.tile([P, P], BF16, tag="xt")
-            nc.tensor.transpose(norm_cols_ps[:], norm_rows[:], ident_bf16[:])
-            nc.vector.tensor_copy(out=norm_cols[:], in_=norm_cols_ps[:, 0 : 2 * PACK])
+        def spread_small_vectors():
+            small_cols = psum_t.tile([P, P], BF16, tag="xt")
+            nc.tensor.transpose(small_cols[:], small_rows[:], ident_bf16[:])
+            nc.scalar.copy(out=bias_cols[:], in_=small_cols[:, 2 * PACK : 2 * PACK + BIAS_ROWS])
+            nc.scalar.copy(out=norm_cols[:], in_=small_cols[:, 0 : 2 * PACK])
 
-        proj_bias = const.tile([P, N_OUT, C], F32)
+        proj_bias = const.tile([P, N_OUT, C], BF16)
 
         def spread_proj_bias():
             for n in range(N_OUT):
-                proj_bias_ps = psum_acc.tile([P, C], F32, tag="acc")
-                nc.tensor.matmul(
-                    proj_bias_ps[:], lhsT=ones[:], rhs=proj_bias_row[:, n * C : (n + 1) * C], start=True, stop=True
-                )
-                nc.scalar.activation(out=proj_bias[:, n, :], in_=proj_bias_ps[:], func=ACT.Copy, scale=OUT_SCALE[n])
+                proj_bias_ps = psum_acc.tile([P, C], BF16, tag="acc")
+                for a in range(ROW_TILES):
+                    r = n * ROW_TILES + a
+                    nc.tensor.matmul(
+                        proj_bias_ps[:, a * P : (a + 1) * P],
+                        lhsT=bias_cols[:, r : r + 1].to_broadcast([P, P]),
+                        rhs=(ident_q if n == 0 else ident_bf16)[:],
+                        start=True,
+                        stop=True,
+                    )
+                nc.scalar.copy(out=proj_bias[:, n, :], in_=proj_bias_ps[:])
 
         w_codes = const.tile([P, N_OUT * C], U32, align_bytes=64)
         w_scales = const.tile([P, N_OUT * C], U8, align_bytes=64)
@@ -153,6 +167,7 @@ def tile_swintransformerblock_pa_t_kernel(
                 in_=w_interleaved[n][:].rearrange("p o t -> p (o t)"),
             )
 
+        means = {}
         negative_means = {}
         rstds = {}
         offsets = {}
@@ -169,11 +184,7 @@ def tile_swintransformerblock_pa_t_kernel(
             mean_var = small.tile([P, GROUP, BN_AGGR_DIM], F32)
             for j in range(GROUP):
                 nc.vector.bn_aggr(out=mean_var[:, j, :], in_=stats[:, j, :])
-            negative_mean = small.tile([P, GROUP], F32)
-            nc.vector.tensor_scalar(
-                out=negative_mean[:], in0=mean_var[:, :, 0], scalar1=-1.0, scalar2=0.0, op0=ALU.mult, op1=ALU.add
-            )
-            negative_means[g] = negative_mean
+            means[g] = mean_var[:, :, 0]
             rstds[g] = small.tile([P, GROUP], F32, name="rstd")
             nc.scalar.activation(
                 out=rstds[g][:], in_=mean_var[:, :, 1], func=ACT.Abs_reciprocal_sqrt, bias=eps[:, 0:1], scale=1.0
@@ -208,7 +219,12 @@ def tile_swintransformerblock_pa_t_kernel(
 
         def offset(g):
             offsets[g] = small.tile([P, GROUP], F32, name="offset")
-            nc.vector.tensor_tensor(out=offsets[g][:], in0=negative_means[g][:], in1=rstds[g][:], op=ALU.mult)
+            if g in means:
+                nc.vector.scalar_tensor_tensor(
+                    out=offsets[g][:], in0=means[g], scalar=-1.0, in1=rstds[g][:], op0=ALU.mult, op1=ALU.mult
+                )
+            else:
+                nc.vector.tensor_tensor(out=offsets[g][:], in0=negative_means[g][:], in1=rstds[g][:], op=ALU.mult)
 
         def normalise(g):
             normed[g] = work.tile([P, GROUP, C], F32, name="xn")
@@ -297,6 +313,8 @@ def tile_swintransformerblock_pa_t_kernel(
                         )
                     nc.sync.dma_start(out=out_views[n][batch][:, place0 : place0 + STORE_TILES, :], in_=result[:])
 
+        spread_small_vectors()
+        spread_proj_bias()
         statistics_on_vector(0)
         offset(0)
         normalise(0)
@@ -304,21 +322,19 @@ def tile_swintransformerblock_pa_t_kernel(
         statistics_on_vector(1)
         offset(1)
         transpose_weights(1)
-        spread_norm_vectors()
         transposes(0)
         gain_and_bias(0)
         normalise(1)
         statistics_on_vector(2)
         quantise_weights(0)
         quantise_weights(1)
-        offset(2)
         transpose_weights(2)
         statistics_on_vector(3)
         interleave(0)
         quantise_weights(2)
         transposes(1)
-        spread_proj_bias()
         quantise(0)
+        offset(2)
 
         for s in range(GROUPS):
             if s + 1 < GROUPS:

import concourse.mybir as mybir
from concourse.masks import make_identity

F32 = mybir.dt.float32
BF16 = mybir.dt.bfloat16
U32 = mybir.dt.uint32
U8 = mybir.dt.uint8
FP8X4 = mybir.dt.float8_e4m3fn_x4
ACT = mybir.ActivationFunctionType
ALU = mybir.AluOpType

P = 128
PACK = 4
C = P * PACK
BATCHES = 4
GRID = 32
WINDOW = 8
SHIFT = 4
WINDOWS = GRID // WINDOW
SLOTS = WINDOW
GROUP = 4
HALVES = SLOTS // GROUP
GROUPS = BATCHES * HALVES
N_OUT = 3
OUT_SCALE = (64.0**-0.5, 1.0, 1.0)
ROW_TILES = C // P
TILES_PER_BANK = 2
BIAS_ROWS = N_OUT * C // P
EPS = 1e-5
BN_STATS_DIM = 6
BN_AGGR_DIM = 2
AHEAD = 4
STORE_TILES = 2
STORE_BUFFERS = 12
ACC_BANKS = 4
QUANTISE_AHEAD = 2

FLOPS = 2 * BATCHES * GRID * GRID * C * N_OUT * C


def tile_swintransformerblock_pa_t_kernel(
    tc, x, ln1_w, ln1_b, in_proj_w, in_proj_b, out_0, out_1, out_2
):
    nc = tc.nc

    x_view = x.rearrange("b (p e) c -> b p e c", e=SLOTS)
    w_view = in_proj_w.rearrange("(a p) k -> p a k", p=P)
    out_views = [
        o.rearrange("w n h d -> (w n) (h d)").rearrange("(b p e) k -> b p e k", b=BATCHES, e=SLOTS)
        for o in (out_0, out_1, out_2)
    ]

    with (
        tc.tile_pool(name="const", bufs=1) as const,
        tc.tile_pool(name="small", bufs=AHEAD) as small,
        tc.tile_pool(name="work", bufs=2) as work,
        tc.tile_pool(name="results", bufs=STORE_BUFFERS) as results,
        tc.psum_pool(name="psum_t", bufs=PACK) as psum_t,
        tc.psum_pool(name="psum_acc", bufs=ACC_BANKS) as psum_acc,
        tc.manual_schedule(),
    ):
        x_tiles = [const.tile([P, GROUP, C], BF16, name="x_%d" % g) for g in range(GROUPS)]
        w_raw = [const.tile([P, ROW_TILES, C], BF16, name="w_raw_%d" % n) for n in range(N_OUT)]

        small_rows = const.tile([P, P], BF16)
        nc.vector.memset(small_rows[:], 0.0)

        def load_x(g, tile0, tiles):
            batch, half = divmod(g, HALVES)
            slot0 = (SHIFT + GROUP * half) % SLOTS + tile0
            nc.sync.dma_start(
                out=x_tiles[g][:, tile0 : tile0 + tiles, :], in_=x_view[batch][:, slot0 : slot0 + tiles, :]
            )

        def load_w(n):
            nc.sync.dma_start(out=w_raw[n][:], in_=w_view[:, n * ROW_TILES : (n + 1) * ROW_TILES, :])

        load_x(0, 0, GROUP // 2)
        nc.sync.dma_start(out=small_rows[0:PACK, :], in_=ln1_w.rearrange("(t p) -> t p", p=P))
        nc.sync.dma_start(out=small_rows[PACK : 2 * PACK, :], in_=ln1_b.rearrange("(t p) -> t p", p=P))
        nc.sync.dma_start(
            out=small_rows[2 * PACK : 2 * PACK + BIAS_ROWS, :], in_=in_proj_b.rearrange("(r p) -> r p", p=P)
        )
        load_x(0, GROUP // 2, GROUP // 2)
        load_w(0)
        load_x(1, 0, GROUP)
        load_w(1)
        load_w(2)
        for g in range(2, GROUPS):
            load_x(g, 0, GROUP)

        ident_f32 = const.tile([P, P], F32)
        make_identity(nc, ident_f32[:])
        ident_bf16 = const.tile([P, P], BF16)
        nc.vector.tensor_copy(out=ident_bf16[:], in_=ident_f32[:])
        ident_q = const.tile([P, P], BF16)
        nc.vector.tensor_scalar(
            out=ident_q[:], in0=ident_f32[:], scalar1=OUT_SCALE[0], scalar2=0.0, op0=ALU.mult, op1=ALU.add
        )
        eps = const.tile([P, 1], F32)
        nc.vector.memset(eps[:], EPS)
        table_warmer = const.tile([P, 1], F32)
        nc.scalar.activation(out=table_warmer[:], in_=eps[:], func=ACT.Abs_reciprocal_sqrt)

        rolled = const.tile([P, P], F32)
        turn = SHIFT * WINDOWS
        nc.vector.tensor_copy(out=rolled[:, 0 : P - turn], in_=ident_f32[:, turn:P])
        nc.vector.tensor_copy(out=rolled[:, P - turn : P], in_=ident_f32[:, 0:turn])
        perm = const.tile([P, HALVES, P], F32)
        rolled_v = rolled[:].rearrange("p (wi r jq) -> p wi jq r", wi=WINDOWS, r=WINDOW)
        perm_0 = perm[:, 0, :].rearrange("p (wi wj r) -> p wi wj r", wi=WINDOWS, r=WINDOW)
        perm_1 = perm[:, 1, :].rearrange("p (wi wj r) -> p wi wj r", wi=WINDOWS, r=WINDOW)
        nc.vector.tensor_copy(out=perm_0, in_=rolled_v)
        nc.vector.tensor_copy(out=perm_1[:, :, 0 : WINDOWS - 1, :], in_=rolled_v[:, :, 1:WINDOWS, :])
        nc.vector.tensor_copy(out=perm_1[:, :, WINDOWS - 1 : WINDOWS, :], in_=rolled_v[:, :, 0:1, :])

        norm_cols = const.tile([P, 2 * PACK], F32)
        bias_cols = const.tile([P, BIAS_ROWS], BF16)

        def spread_small_vectors():
            small_cols = psum_t.tile([P, P], BF16, tag="xt")
            nc.tensor.transpose(small_cols[:], small_rows[:], ident_bf16[:])
            nc.scalar.copy(out=bias_cols[:], in_=small_cols[:, 2 * PACK : 2 * PACK + BIAS_ROWS])
            nc.scalar.copy(out=norm_cols[:], in_=small_cols[:, 0 : 2 * PACK])

        proj_bias = const.tile([P, N_OUT, C], BF16)

        def spread_proj_bias():
            for n in range(N_OUT):
                proj_bias_ps = psum_acc.tile([P, C], BF16, tag="acc")
                for a in range(ROW_TILES):
                    r = n * ROW_TILES + a
                    nc.tensor.matmul(
                        proj_bias_ps[:, a * P : (a + 1) * P],
                        lhsT=bias_cols[:, r : r + 1].to_broadcast([P, P]),
                        rhs=(ident_q if n == 0 else ident_bf16)[:],
                        start=True,
                        stop=True,
                    )
                nc.scalar.copy(out=proj_bias[:, n, :], in_=proj_bias_ps[:])

        w_codes = const.tile([P, N_OUT * C], U32, align_bytes=64)
        w_scales = const.tile([P, N_OUT * C], U8, align_bytes=64)
        w_interleaved = {}

        def transpose_weights(n):
            w_interleaved[n] = work.tile([P, C, PACK], BF16, align_bytes=64, name="w_interleaved")
            for bank in range(ROW_TILES // TILES_PER_BANK):
                wt = psum_acc.tile([P, TILES_PER_BANK, PACK, P], BF16, tag="acc")
                for a in range(TILES_PER_BANK):
                    for t in range(PACK):
                        nc.tensor.transpose(
                            wt[:, a, t, :], w_raw[n][:, TILES_PER_BANK * bank + a, t * P : (t + 1) * P], ident_bf16[:]
                        )
                rows = TILES_PER_BANK * P
                nc.scalar.copy(
                    out=w_interleaved[n][:, bank * rows : (bank + 1) * rows, :].rearrange(
                        "p (a o) t -> p a o t", a=TILES_PER_BANK
                    ),
                    in_=wt[:].rearrange("p a t o -> p a o t"),
                )

        def quantise_weights(n):
            nc.vector.quantize_mx(
                out=w_codes[:, n * C : (n + 1) * C].bitcast(FP8X4),
                scales=w_scales[:, n * C : (n + 1) * C],
                in_=w_interleaved[n][:].rearrange("p o t -> p (o t)"),
            )

        means = {}
        negative_means = {}
        rstds = {}
        offsets = {}
        normed = {}
        banks = {}
        chunks = {}
        interleaved = {}
        quantised = {}

        def statistics_on_vector(g):
            stats = small.tile([P, GROUP, BN_STATS_DIM], F32)
            for j in range(GROUP):
                nc.vector.bn_stats(out=stats[:, j, :], in_=x_tiles[g][:, j, :])
            mean_var = small.tile([P, GROUP, BN_AGGR_DIM], F32)
            for j in range(GROUP):
                nc.vector.bn_aggr(out=mean_var[:, j, :], in_=stats[:, j, :])
            means[g] = mean_var[:, :, 0]
            rstds[g] = small.tile([P, GROUP], F32, name="rstd")
            nc.scalar.activation(
                out=rstds[g][:], in_=mean_var[:, :, 1], func=ACT.Abs_reciprocal_sqrt, bias=eps[:, 0:1], scale=1.0
            )

        def statistics_on_scalar(g):
            unread = work.tile([P, 2 * GROUP, C], BF16, bufs=1)
            negative_mean = small.tile([P, GROUP], F32)
            for j in range(GROUP):
                nc.scalar.activation(
                    out=unread[:, j, :],
                    in_=x_tiles[g][:, j, :],
                    func=ACT.Identity,
                    scale=-1.0 / C,
                    accum_out=negative_mean[:, j : j + 1],
                )
            squares = small.tile([P, GROUP], F32)
            for j in range(GROUP):
                nc.scalar.activation(
                    out=unread[:, GROUP + j, :],
                    in_=x_tiles[g][:, j, :],
                    func=ACT.Square,
                    scale=1.0,
                    bias=negative_mean[:, j : j + 1],
                    accum_out=squares[:, j : j + 1],
                )
            negative_means[g] = negative_mean
            rstds[g] = small.tile([P, GROUP], F32, name="rstd")
            nc.scalar.activation(
                out=rstds[g][:], in_=squares[:], func=ACT.Abs_reciprocal_sqrt, bias=eps[:, 0:1], scale=1.0 / C
            )

        def offset(g):
            offsets[g] = small.tile([P, GROUP], F32, name="offset")
            if g in means:
                nc.vector.scalar_tensor_tensor(
                    out=offsets[g][:], in0=means[g], scalar=-1.0, in1=rstds[g][:], op0=ALU.mult, op1=ALU.mult
                )
            else:
                nc.vector.tensor_tensor(out=offsets[g][:], in0=negative_means[g][:], in1=rstds[g][:], op=ALU.mult)

        def normalise(g):
            normed[g] = work.tile([P, GROUP, C], F32, name="xn")
            for j in range(GROUP):
                nc.gpsimd.tensor_scalar(
                    out=normed[g][:, j, :],
                    in0=x_tiles[g][:, j, :],
                    scalar1=rstds[g][:, j : j + 1],
                    scalar2=offsets[g][:, j : j + 1],
                    op0=ALU.mult,
                    op1=ALU.add,
                )

        def transposes(g):
            half = g % HALVES
            banks[g] = []
            for t in range(PACK):
                xt = psum_t.tile([P, GROUP, P], F32, tag="xt")
                for j in range(GROUP):
                    nc.tensor.transpose(xt[:, j, :], normed[g][:, j, t * P : (t + 1) * P], perm[:, half, :])
                banks[g].append(xt)

        def gain_and_bias(g):
            chunks[g] = work.tile([P, PACK, GROUP * P], BF16, name="h_chunks")
            for t in range(PACK):
                nc.scalar.activation(
                    out=chunks[g][:, t, :],
                    in_=banks[g][t][:].rearrange("p j m -> p (j m)"),
                    func=ACT.Identity,
                    scale=norm_cols[:, t : t + 1],
                    bias=norm_cols[:, PACK + t : PACK + t + 1],
                )

        def interleave(g):
            interleaved[g] = work.tile([P, GROUP * P, PACK], BF16, align_bytes=64, name="h_interleaved")
            nc.gpsimd.tensor_scalar(
                out=interleaved[g][:],
                in0=chunks[g][:].rearrange("p t m -> p m t"),
                scalar1=1.0,
                scalar2=0.0,
                op0=ALU.mult,
                op1=ALU.add,
            )

        def quantise(g):
            codes = work.tile([P, GROUP * P], U32, align_bytes=64)
            scales = work.tile([P, GROUP * P], U8, align_bytes=64)
            nc.vector.quantize_mx(
                out=codes[:].bitcast(FP8X4), scales=scales[:], in_=interleaved[g][:].rearrange("p m t -> p (m t)")
            )
            quantised[g] = (codes, scales)

        def project(g):
            batch, half = divmod(g, HALVES)
            codes, scales = quantised[g]
            left = GROUP * N_OUT
            for tile0 in range(0, GROUP, STORE_TILES):
                place0 = GROUP * half + tile0
                for n in range(N_OUT):
                    result = results.tile([P, STORE_TILES, C], F32)
                    for i in range(STORE_TILES):
                        j = tile0 + i
                        if left == QUANTISE_AHEAD:
                            if g + 1 < GROUPS:
                                quantise(g + 1)
                            if g + AHEAD - 1 < GROUPS:
                                offset(g + AHEAD - 1)
                        left -= 1
                        acc = psum_acc.tile([P, C], F32, tag="acc")
                        nc.tensor.matmul_mx(
                            out=acc[:],
                            lhsT=codes[:, j * P : (j + 1) * P].bitcast(FP8X4),
                            lhsT_scale=scales[:, j * P : (j + 1) * P],
                            rhs=w_codes[:, n * C : (n + 1) * C].bitcast(FP8X4),
                            rhs_scale=w_scales[:, n * C : (n + 1) * C],
                            start=True,
                            stop=True,
                        )
                        nc.vector.scalar_tensor_tensor(
                            out=result[:, i, :],
                            in0=acc[:],
                            scalar=OUT_SCALE[n],
                            in1=proj_bias[:, n, :],
                            op0=ALU.mult,
                            op1=ALU.add,
                        )
                    nc.sync.dma_start(out=out_views[n][batch][:, place0 : place0 + STORE_TILES, :], in_=result[:])

        spread_small_vectors()
        spread_proj_bias()
        statistics_on_vector(0)
        offset(0)
        normalise(0)
        transpose_weights(0)
        statistics_on_vector(1)
        offset(1)
        transpose_weights(1)
        transposes(0)
        gain_and_bias(0)
        normalise(1)
        statistics_on_vector(2)
        quantise_weights(0)
        quantise_weights(1)
        transpose_weights(2)
        statistics_on_vector(3)
        interleave(0)
        quantise_weights(2)
        transposes(1)
        quantise(0)
        offset(2)

        for s in range(GROUPS):
            if s + 1 < GROUPS:
                gain_and_bias(s + 1)
            if s + 2 < GROUPS:
                normalise(s + 2)
            if s + 1 < GROUPS:
                interleave(s + 1)
            project(s)
            if s + AHEAD < GROUPS:
                statistics_on_scalar(s + AHEAD)
            if s + 2 < GROUPS:
                transposes(s + 2)
